import numpy as np
import ml_dtypes

BF16 = ml_dtypes.bfloat16


def bf(x):
    return np.asarray(x, np.float32).astype(BF16)


def f32(x):
    return np.asarray(x, np.float32)


def f64(x):
    return np.asarray(x).astype(np.float64)


def striped(idx):
    return np.tile(idx.reshape(-1, 16).T, (8, 1))


B, NB, T, S, G, CW, C, N = 2, 8, 32, 512, 64, 5, 512, 320
BN_EPS = 1e-5
MAXNORM = 2.0
TINY = 1e-7


def rows(a):
    return f32(np.tile(np.repeat(a, T, axis=0), (B, 1)))


def setup_inputs():
    return {"x": f32(np.random.standard_normal((C, S))), "w": rows(np.random.standard_normal((NB, N))), "conv_b": rows(0.1 * np.random.standard_normal((NB, G))), "bn_gamma": rows(1.0 + 0.1 * np.random.standard_normal((NB, G))), "bn_beta": rows(0.1 * np.random.standard_normal((NB, G))), "bn_mean": rows(0.1 * np.random.standard_normal((NB, G))), "bn_var": rows(np.random.uniform(0.5, 1.5, (NB, G))), "offs": striped(np.random.permutation(np.tile(np.arange(S), 2))[:N])}


def reference(x, w, conv_b, bn_gamma, bn_beta, bn_mean, bn_var, offs):
    idx = offs[:16].T.reshape(-1)
    wf = f64(w).reshape(C, G, CW)
    nrm = np.sqrt(np.sum(wf * wf, axis=2, keepdims=True))
    wn = (wf * np.where(nrm > MAXNORM, MAXNORM / (nrm + TINY), 1.0)).reshape(C, N)
    z = (f64(x)[:, idx] * wn).reshape(C, G, CW).sum(axis=2) + f64(conv_b)
    y = (z - f64(bn_mean)) * (f64(bn_gamma) / np.sqrt(f64(bn_var) + BN_EPS)) + f64(bn_beta)
    return y / (1.0 + np.exp(-y))

@@ -1,0 +1,98 @@
+import concourse.mybir as mybir
+
+F32 = mybir.dt.float32
+U16 = mybir.dt.uint16
+ALU = mybir.AluOpType
+ACT = mybir.ActivationFunctionType
+AXIS = mybir.AxisListType
+
+P = 128
+TRIALS = 2
+HALVES = 2
+BANDS = 8
+ELECTRODES = 512
+GROUPS = 64
+PICKS = 5
+N = GROUPS * PICKS
+BN_EPS = 1e-5
+
+BYTES = (
+    TRIALS * HALVES * P * ELECTRODES * 4
+    + BANDS * (N + 5 * GROUPS) * 4
+    + P * (N // 16) * 2
+    + TRIALS * HALVES * P * GROUPS * 4
+)
+
+
+def by_half(ap):
+    return ap.rearrange("p (h n) -> p h n", h=HALVES)
+
+
+def by_group(ap):
+    return ap.rearrange("p (q k) -> p q k", k=PICKS)
+
+
+def tile_se_fbcnet_kernel(tc, x, w, conv_b, bn_gamma, bn_beta, bn_mean, bn_var, offs, out):
+    nc = tc.nc
+    with tc.tile_pool(name="held", bufs=1) as held, tc.tile_pool(name="work", bufs=2) as work:
+        offsets = held.tile([P, N // 16], U16, name="offsets")
+        nc.sync.dma_start(offsets[:], offs)
+
+        weights = held.tile([P, HALVES * N], F32, name="weights")
+        windows = [held.tile([P, ELECTRODES], F32, name=f"window{i}") for i in range(TRIALS * HALVES)]
+        for h in range(HALVES):
+            nc.sync.dma_start(weights[:, h * N : (h + 1) * N], w[h * P : (h + 1) * P, :])
+            nc.sync.dma_start(windows[h][:], x[h * P : (h + 1) * P, :])
+        for i in range(HALVES, TRIALS * HALVES):
+            nc.sync.dma_start(windows[i][:], x[i * P : (i + 1) * P, :])
+
+        tables = {}
+        for name, table in (
+            ("var", bn_var),
+            ("gamma", bn_gamma),
+            ("mean", bn_mean),
+            ("conv_b", conv_b),
+            ("beta", bn_beta),
+        ):
+            tables[name] = held.tile([P, HALVES * GROUPS], F32, name=name)
+            nc.scalar.dma_start(
+                by_half(tables[name][:]),
+                table[0 : HALVES * P, :].rearrange("(h p) g -> p h g", p=P),
+            )
+
+        squares = held.tile([P, HALVES * N], F32, name="squares")
+        nc.scalar.activation(squares[:], weights[:], ACT.Square)
+        limit = held.tile([P, HALVES * GROUPS], F32, name="limit")
+        nc.vector.tensor_reduce(limit[:], by_group(squares[:]), axis=AXIS.X, op=ALU.add)
+        nc.vector.tensor_scalar(limit[:], limit[:], 0.25, 1.0, op0=ALU.mult, op1=ALU.max)
+        nc.scalar.activation(limit[:], limit[:], ACT.Abs_reciprocal_sqrt)
+
+        gain = held.tile([P, HALVES * GROUPS], F32, name="gain")
+        nc.scalar.activation(gain[:], tables["var"][:], ACT.Abs_reciprocal_sqrt, bias=BN_EPS)
+        nc.vector.tensor_mul(gain[:], gain[:], tables["gamma"][:])
+        scale = held.tile([P, HALVES * GROUPS], F32, name="scale")
+        nc.vector.tensor_mul(scale[:], limit[:], gain[:])
+        shift = held.tile([P, HALVES * GROUPS], F32, name="shift")
+        nc.vector.tensor_sub(shift[:], tables["conv_b"][:], tables["mean"][:])
+        nc.vector.tensor_mul(shift[:], shift[:], gain[:])
+        nc.vector.tensor_add(shift[:], shift[:], tables["beta"][:])
+
+        for b in range(TRIALS):
+            products = work.tile([P, HALVES * N], F32, name="products")
+            for h in range(HALVES):
+                nc.vector.tensor_tensor(
+                    products[:, h * N : (h + 1) * N],
+                    windows[b * HALVES + h][:].indirect(offsets[:]),
+                    weights[:, h * N : (h + 1) * N],
+                    ALU.mult,
+                )
+            normed = work.tile([P, HALVES * GROUPS], F32, name="normed")
+            nc.vector.tensor_reduce(normed[:], by_group(products[:]), axis=AXIS.X, op=ALU.add)
+            nc.vector.tensor_mul(normed[:], normed[:], scale[:])
+            nc.vector.tensor_add(normed[:], normed[:], shift[:])
+            swish = work.tile([P, HALVES * GROUPS], F32, name="swish")
+            nc.scalar.activation(swish[:], normed[:], ACT.Silu)
+            nc.scalar.dma_start(
+                out[b * HALVES * P : (b + 1) * HALVES * P, :].rearrange("(h p) g -> p h g", p=P),
+                by_half(swish[:]),
+            )

@@ -10,12 +10,14 @@ P = 128
 TRIALS = 2
 HALVES = 2
 BANDS = 8
+SAMPLES = 32
 ELECTRODES = 512
 GROUPS = 64
 PICKS = 5
 N = GROUPS * PICKS
 BN_EPS = 1e-5
 
+FLOPS = 2 * TRIALS * HALVES * P * N
 BYTES = (
     TRIALS * HALVES * P * ELECTRODES * 4
     + BANDS * (N + 5 * GROUPS) * 4
@@ -32,9 +34,17 @@ def by_group(ap):
     return ap.rearrange("p (q k) -> p q k", k=PICKS)
 
 
+def band_rows(table):
+    return table[0 : BANDS * SAMPLES, :].rearrange("(k t) n -> k t n", t=SAMPLES)[:, 0, :]
+
+
 def tile_se_fbcnet_kernel(tc, x, w, conv_b, bn_gamma, bn_beta, bn_mean, bn_var, offs, out):
     nc = tc.nc
-    with tc.tile_pool(name="held", bufs=1) as held, tc.tile_pool(name="work", bufs=2) as work:
+    with (
+        tc.tile_pool(name="held", bufs=1) as held,
+        tc.tile_pool(name="work", bufs=2) as work,
+        tc.psum_pool(name="psum", bufs=1) as psum,
+    ):
         offsets = held.tile([P, N // 16], U16, name="offsets")
         nc.sync.dma_start(offsets[:], offs)
 
@@ -46,36 +56,57 @@ def tile_se_fbcnet_kernel(tc, x, w, conv_b, bn_gamma, bn_beta, bn_mean, bn_var, 
         for i in range(HALVES, TRIALS * HALVES):
             nc.sync.dma_start(windows[i][:], x[i * P : (i + 1) * P, :])
 
-        tables = {}
-        for name, table in (
-            ("var", bn_var),
-            ("gamma", bn_gamma),
-            ("mean", bn_mean),
-            ("conv_b", conv_b),
-            ("beta", bn_beta),
-        ):
-            tables[name] = held.tile([P, HALVES * GROUPS], F32, name=name)
-            nc.scalar.dma_start(
-                by_half(tables[name][:]),
-                table[0 : HALVES * P, :].rearrange("(h p) g -> p h g", p=P),
+        band_w = held.tile([BANDS, N], F32, name="band_w")
+        var = held.tile([BANDS, GROUPS], F32, name="var")
+        factor = held.tile([BANDS, 2 * GROUPS], F32, name="factor")
+        bias = held.tile([BANDS, GROUPS], F32, name="bias")
+        mean = held.tile([BANDS, GROUPS], F32, name="mean")
+        beta = held.tile([BANDS, GROUPS], F32, name="beta")
+        nc.scalar.dma_start(band_w[:], band_rows(w))
+        nc.scalar.dma_start(var[:], band_rows(bn_var))
+        nc.scalar.dma_start(factor[:, 0:GROUPS], band_rows(bn_gamma))
+        nc.gpsimd.dma_start(bias[:], band_rows(conv_b))
+        nc.gpsimd.dma_start(mean[:], band_rows(bn_mean))
+        nc.gpsimd.dma_start(beta[:], band_rows(bn_beta))
+
+        spread = held.tile([BANDS, HALVES * P], F32, name="spread")
+        nc.gpsimd.memset(spread[:], 1.0)
+        nc.gpsimd.affine_select(
+            out=spread[:], in_=spread[:], compare_op=ALU.is_ge, fill=0.0,
+            base=0, pattern=[[1, HALVES * P]], channel_multiplier=-SAMPLES,
+        )
+        nc.gpsimd.affine_select(
+            out=spread[:], in_=spread[:], compare_op=ALU.is_ge, fill=0.0,
+            base=SAMPLES - 1, pattern=[[-1, HALVES * P]], channel_multiplier=SAMPLES,
+        )
+
+        nc.gpsimd.tensor_sub(bias[:], bias[:], mean[:])
+        nc.gpsimd.tensor_mul(factor[:, GROUPS : 2 * GROUPS], bias[:], factor[:, 0:GROUPS])
+
+        inside = held.tile([BANDS, 2 * GROUPS], F32, name="inside")
+        squares = held.tile([BANDS, N], F32, name="squares")
+        nc.vector.tensor_mul(squares[:], band_w[:], band_w[:])
+        nc.vector.tensor_reduce(inside[:, 0:GROUPS], by_group(squares[:]), axis=AXIS.X, op=ALU.add)
+        nc.vector.tensor_scalar_add(inside[:, GROUPS : 2 * GROUPS], var[:], BN_EPS)
+        nc.vector.tensor_scalar(inside[:, 0:GROUPS], inside[:, 0:GROUPS], 0.25, 1.0, op0=ALU.mult, op1=ALU.max)
+        nc.vector.tensor_mul(inside[:, 0:GROUPS], inside[:, 0:GROUPS], inside[:, GROUPS : 2 * GROUPS])
+
+        band_affine = held.tile([BANDS, 2 * GROUPS], F32, name="band_affine")
+        nc.scalar.activation(band_affine[:], inside[:], ACT.Abs_reciprocal_sqrt)
+        nc.vector.tensor_mul(band_affine[:], band_affine[:], factor[:])
+        nc.vector.tensor_add(band_affine[:, GROUPS : 2 * GROUPS], band_affine[:, GROUPS : 2 * GROUPS], beta[:])
+
+        affine = psum.tile([P, 2 * HALVES * GROUPS], F32, name="affine")
+        for h in range(HALVES):
+            nc.tensor.matmul(
+                affine[:].rearrange("p (a h q) -> p a h q", a=2, h=HALVES)[:, :, h, :],
+                lhsT=spread[:, h * P : (h + 1) * P],
+                rhs=band_affine[:].rearrange("k (a q) -> k a q", a=2),
+                start=True,
+                stop=True,
             )
-
-        squares = held.tile([P, HALVES * N], F32, name="squares")
-        nc.scalar.activation(squares[:], weights[:], ACT.Square)
-        limit = held.tile([P, HALVES * GROUPS], F32, name="limit")
-        nc.vector.tensor_reduce(limit[:], by_group(squares[:]), axis=AXIS.X, op=ALU.add)
-        nc.vector.tensor_scalar(limit[:], limit[:], 0.25, 1.0, op0=ALU.mult, op1=ALU.max)
-        nc.scalar.activation(limit[:], limit[:], ACT.Abs_reciprocal_sqrt)
-
-        gain = held.tile([P, HALVES * GROUPS], F32, name="gain")
-        nc.scalar.activation(gain[:], tables["var"][:], ACT.Abs_reciprocal_sqrt, bias=BN_EPS)
-        nc.vector.tensor_mul(gain[:], gain[:], tables["gamma"][:])
-        scale = held.tile([P, HALVES * GROUPS], F32, name="scale")
-        nc.vector.tensor_mul(scale[:], limit[:], gain[:])
-        shift = held.tile([P, HALVES * GROUPS], F32, name="shift")
-        nc.vector.tensor_sub(shift[:], tables["conv_b"][:], tables["mean"][:])
-        nc.vector.tensor_mul(shift[:], shift[:], gain[:])
-        nc.vector.tensor_add(shift[:], shift[:], tables["beta"][:])
+        scale = affine[:, 0 : HALVES * GROUPS]
+        shift = affine[:, HALVES * GROUPS : 2 * HALVES * GROUPS]
 
         for b in range(TRIALS):
             products = work.tile([P, HALVES * N], F32, name="products")
@@ -88,8 +119,8 @@ def tile_se_fbcnet_kernel(tc, x, w, conv_b, bn_gamma, bn_beta, bn_mean, bn_var, 
                 )
             normed = work.tile([P, HALVES * GROUPS], F32, name="normed")
             nc.vector.tensor_reduce(normed[:], by_group(products[:]), axis=AXIS.X, op=ALU.add)
-            nc.vector.tensor_mul(normed[:], normed[:], scale[:])
-            nc.vector.tensor_add(normed[:], normed[:], shift[:])
+            nc.vector.tensor_mul(normed[:], normed[:], scale)
+            nc.vector.tensor_add(normed[:], normed[:], shift)
             swish = work.tile([P, HALVES * GROUPS], F32, name="swish")
             nc.scalar.activation(swish[:], normed[:], ACT.Silu)
             nc.scalar.dma_start(

@@ -8,122 +8,99 @@ AXIS = mybir.AxisListType
 
 P = 128
 TRIALS = 2
-HALVES = 2
+PARITIES = 2
 BANDS = 8
-SAMPLES = 32
 ELECTRODES = 512
 GROUPS = 64
 PICKS = 5
 N = GROUPS * PICKS
 BN_EPS = 1e-5
 
-FLOPS = 2 * TRIALS * HALVES * P * N
 BYTES = (
-    TRIALS * HALVES * P * ELECTRODES * 4
+    TRIALS * PARITIES * P * ELECTRODES * 4
     + BANDS * (N + 5 * GROUPS) * 4
     + P * (N // 16) * 2
-    + TRIALS * HALVES * P * GROUPS * 4
+    + TRIALS * PARITIES * P * GROUPS * 4
 )
 
 
-def by_half(ap):
-    return ap.rearrange("p (h n) -> p h n", h=HALVES)
+def block(table, b, i):
+    return table.rearrange("(b p i) n -> b i p n", b=TRIALS, i=PARITIES)[b, i]
 
 
 def by_group(ap):
     return ap.rearrange("p (q k) -> p q k", k=PICKS)
 
 
-def band_rows(table):
-    return table[0 : BANDS * SAMPLES, :].rearrange("(k t) n -> k t n", t=SAMPLES)[:, 0, :]
+def by_parity(ap):
+    return ap.rearrange("p (i q) -> p i q", i=PARITIES)
+
+
+def for_both(ap):
+    return ap.unsqueeze(1).to_broadcast([P, PARITIES, GROUPS])
 
 
 def tile_se_fbcnet_kernel(tc, x, w, conv_b, bn_gamma, bn_beta, bn_mean, bn_var, offs, out):
     nc = tc.nc
-    with (
-        tc.tile_pool(name="held", bufs=1) as held,
-        tc.tile_pool(name="work", bufs=2) as work,
-        tc.psum_pool(name="psum", bufs=1) as psum,
-    ):
+    with tc.tile_pool(name="held", bufs=1) as held, tc.tile_pool(name="work", bufs=2) as work:
         offsets = held.tile([P, N // 16], U16, name="offsets")
+        weights = held.tile([P, N], F32, name="weights")
+        windows = [
+            [held.tile([P, ELECTRODES], F32, name=f"window{b}{i}") for i in range(PARITIES)]
+            for b in range(TRIALS)
+        ]
+        var = held.tile([P, GROUPS], F32, name="var")
+        gamma = held.tile([P, GROUPS], F32, name="gamma")
+        bias = held.tile([P, GROUPS], F32, name="bias")
+        mean = held.tile([P, GROUPS], F32, name="mean")
+        beta = held.tile([P, GROUPS], F32, name="beta")
+
+        nc.scalar.dma_start(weights[:], block(w, 0, 0))
+        nc.scalar.dma_start(var[:], block(bn_var, 0, 0))
+        nc.scalar.dma_start(gamma[:], block(bn_gamma, 0, 0))
+        nc.scalar.dma_start(bias[:], block(conv_b, 0, 0))
+
         nc.sync.dma_start(offsets[:], offs)
+        nc.sync.dma_start(windows[0][0][:], block(x, 0, 0))
+        nc.sync.dma_start(windows[0][1][:], block(x, 0, 1))
+        nc.sync.dma_start(mean[:], block(bn_mean, 0, 0))
+        nc.sync.dma_start(windows[1][0][:], block(x, 1, 0))
+        nc.sync.dma_start(windows[1][1][:], block(x, 1, 1))
+        nc.sync.dma_start(beta[:], block(bn_beta, 0, 0))
 
-        weights = held.tile([P, HALVES * N], F32, name="weights")
-        windows = [held.tile([P, ELECTRODES], F32, name=f"window{i}") for i in range(TRIALS * HALVES)]
-        for h in range(HALVES):
-            nc.sync.dma_start(weights[:, h * N : (h + 1) * N], w[h * P : (h + 1) * P, :])
-            nc.sync.dma_start(windows[h][:], x[h * P : (h + 1) * P, :])
-        for i in range(HALVES, TRIALS * HALVES):
-            nc.sync.dma_start(windows[i][:], x[i * P : (i + 1) * P, :])
+        squares = held.tile([P, N], F32, name="squares")
+        nc.scalar.activation(squares[:], weights[:], ACT.Square)
+        limit = held.tile([P, GROUPS], F32, name="limit")
+        nc.vector.tensor_reduce(limit[:], by_group(squares[:]), axis=AXIS.X, op=ALU.add)
+        nc.vector.tensor_scalar(limit[:], limit[:], 0.25, 1.0, op0=ALU.mult, op1=ALU.max)
+        nc.scalar.activation(limit[:], limit[:], ACT.Abs_reciprocal_sqrt)
 
-        band_w = held.tile([BANDS, N], F32, name="band_w")
-        var = held.tile([BANDS, GROUPS], F32, name="var")
-        factor = held.tile([BANDS, 2 * GROUPS], F32, name="factor")
-        bias = held.tile([BANDS, GROUPS], F32, name="bias")
-        mean = held.tile([BANDS, GROUPS], F32, name="mean")
-        beta = held.tile([BANDS, GROUPS], F32, name="beta")
-        nc.scalar.dma_start(band_w[:], band_rows(w))
-        nc.scalar.dma_start(var[:], band_rows(bn_var))
-        nc.scalar.dma_start(factor[:, 0:GROUPS], band_rows(bn_gamma))
-        nc.gpsimd.dma_start(bias[:], band_rows(conv_b))
-        nc.gpsimd.dma_start(mean[:], band_rows(bn_mean))
-        nc.gpsimd.dma_start(beta[:], band_rows(bn_beta))
-
-        spread = held.tile([BANDS, HALVES * P], F32, name="spread")
-        nc.gpsimd.memset(spread[:], 1.0)
-        nc.gpsimd.affine_select(
-            out=spread[:], in_=spread[:], compare_op=ALU.is_ge, fill=0.0,
-            base=0, pattern=[[1, HALVES * P]], channel_multiplier=-SAMPLES,
-        )
-        nc.gpsimd.affine_select(
-            out=spread[:], in_=spread[:], compare_op=ALU.is_ge, fill=0.0,
-            base=SAMPLES - 1, pattern=[[-1, HALVES * P]], channel_multiplier=SAMPLES,
-        )
-
-        nc.gpsimd.tensor_sub(bias[:], bias[:], mean[:])
-        nc.gpsimd.tensor_mul(factor[:, GROUPS : 2 * GROUPS], bias[:], factor[:, 0:GROUPS])
-
-        inside = held.tile([BANDS, 2 * GROUPS], F32, name="inside")
-        squares = held.tile([BANDS, N], F32, name="squares")
-        nc.vector.tensor_mul(squares[:], band_w[:], band_w[:])
-        nc.vector.tensor_reduce(inside[:, 0:GROUPS], by_group(squares[:]), axis=AXIS.X, op=ALU.add)
-        nc.vector.tensor_scalar_add(inside[:, GROUPS : 2 * GROUPS], var[:], BN_EPS)
-        nc.vector.tensor_scalar(inside[:, 0:GROUPS], inside[:, 0:GROUPS], 0.25, 1.0, op0=ALU.mult, op1=ALU.max)
-        nc.vector.tensor_mul(inside[:, 0:GROUPS], inside[:, 0:GROUPS], inside[:, GROUPS : 2 * GROUPS])
-
-        band_affine = held.tile([BANDS, 2 * GROUPS], F32, name="band_affine")
-        nc.scalar.activation(band_affine[:], inside[:], ACT.Abs_reciprocal_sqrt)
-        nc.vector.tensor_mul(band_affine[:], band_affine[:], factor[:])
-        nc.vector.tensor_add(band_affine[:, GROUPS : 2 * GROUPS], band_affine[:, GROUPS : 2 * GROUPS], beta[:])
-
-        affine = psum.tile([P, 2 * HALVES * GROUPS], F32, name="affine")
-        for h in range(HALVES):
-            nc.tensor.matmul(
-                affine[:].rearrange("p (a h q) -> p a h q", a=2, h=HALVES)[:, :, h, :],
-                lhsT=spread[:, h * P : (h + 1) * P],
-                rhs=band_affine[:].rearrange("k (a q) -> k a q", a=2),
-                start=True,
-                stop=True,
-            )
-        scale = affine[:, 0 : HALVES * GROUPS]
-        shift = affine[:, HALVES * GROUPS : 2 * HALVES * GROUPS]
+        gain = held.tile([P, GROUPS], F32, name="gain")
+        nc.scalar.activation(gain[:], var[:], ACT.Abs_reciprocal_sqrt, bias=BN_EPS)
+        nc.vector.tensor_mul(gain[:], gain[:], gamma[:])
+        scale = held.tile([P, GROUPS], F32, name="scale")
+        nc.vector.tensor_mul(scale[:], limit[:], gain[:])
+        shift = held.tile([P, GROUPS], F32, name="shift")
+        nc.vector.tensor_sub(shift[:], bias[:], mean[:])
+        nc.vector.tensor_mul(shift[:], shift[:], gain[:])
+        nc.vector.tensor_add(shift[:], shift[:], beta[:])
 
         for b in range(TRIALS):
-            products = work.tile([P, HALVES * N], F32, name="products")
-            for h in range(HALVES):
+            products = work.tile([P, PARITIES * N], F32, name="products")
+            for i in range(PARITIES):
                 nc.vector.tensor_tensor(
-                    products[:, h * N : (h + 1) * N],
-                    windows[b * HALVES + h][:].indirect(offsets[:]),
-                    weights[:, h * N : (h + 1) * N],
+                    products[:, i * N : (i + 1) * N],
+                    windows[b][i][:].indirect(offsets[:]),
+                    weights[:],
                     ALU.mult,
                 )
-            normed = work.tile([P, HALVES * GROUPS], F32, name="normed")
+            normed = work.tile([P, PARITIES * GROUPS], F32, name="normed")
             nc.vector.tensor_reduce(normed[:], by_group(products[:]), axis=AXIS.X, op=ALU.add)
-            nc.vector.tensor_mul(normed[:], normed[:], scale)
-            nc.vector.tensor_add(normed[:], normed[:], shift)
-            swish = work.tile([P, HALVES * GROUPS], F32, name="swish")
+            nc.vector.tensor_tensor(by_parity(normed[:]), by_parity(normed[:]), for_both(scale[:]), ALU.mult)
+            nc.vector.tensor_tensor(by_parity(normed[:]), by_parity(normed[:]), for_both(shift[:]), ALU.add)
+            swish = work.tile([P, PARITIES * GROUPS], F32, name="swish")
             nc.scalar.activation(swish[:], normed[:], ACT.Silu)
             nc.scalar.dma_start(
-                out[b * HALVES * P : (b + 1) * HALVES * P, :].rearrange("(h p) g -> p h g", p=P),
-                by_half(swish[:]),
+                out[b * PARITIES * P : (b + 1) * PARITIES * P, :].rearrange("(p i) q -> p (i q)", i=PARITIES),
+                swish[:],
             )

@@ -1,4 +1,5 @@
 import concourse.mybir as mybir
+from concourse.masks import make_identity
 
 F32 = mybir.dt.float32
 U16 = mybir.dt.uint16
@@ -16,6 +17,7 @@ PICKS = 5
 N = GROUPS * PICKS
 BN_EPS = 1e-5
 
+FLOPS = 2 * TRIALS * PARITIES * P * N
 BYTES = (
     TRIALS * PARITIES * P * ELECTRODES * 4
     + BANDS * (N + 5 * GROUPS) * 4
@@ -42,7 +44,11 @@ def for_both(ap):
 
 def tile_se_fbcnet_kernel(tc, x, w, conv_b, bn_gamma, bn_beta, bn_mean, bn_var, offs, out):
     nc = tc.nc
-    with tc.tile_pool(name="held", bufs=1) as held, tc.tile_pool(name="work", bufs=2) as work:
+    with (
+        tc.tile_pool(name="held", bufs=1) as held,
+        tc.tile_pool(name="work", bufs=2) as work,
+        tc.psum_pool(name="psum", bufs=1) as psum,
+    ):
         offsets = held.tile([P, N // 16], U16, name="offsets")
         weights = held.tile([P, N], F32, name="weights")
         windows = [
@@ -67,6 +73,9 @@ def tile_se_fbcnet_kernel(tc, x, w, conv_b, bn_gamma, bn_beta, bn_mean, bn_var, 
         nc.sync.dma_start(windows[1][0][:], block(x, 1, 0))
         nc.sync.dma_start(windows[1][1][:], block(x, 1, 1))
         nc.sync.dma_start(beta[:], block(bn_beta, 0, 0))
+
+        identity = held.tile([P, P], F32, name="identity")
+        make_identity(nc, identity[:])
 
         squares = held.tile([P, N], F32, name="squares")
         nc.scalar.activation(squares[:], weights[:], ACT.Square)
@@ -94,9 +103,21 @@ def tile_se_fbcnet_kernel(tc, x, w, conv_b, bn_gamma, bn_beta, bn_mean, bn_var, 
                     weights[:],
                     ALU.mult,
                 )
+            if b < TRIALS - 1:
+                sums = psum.tile([P, PARITIES * GROUPS], F32, name="sums_psum")
+                for k in range(PICKS):
+                    nc.tensor.matmul(
+                        sums[:],
+                        lhsT=identity[:],
+                        rhs=by_group(products[:])[:, :, k],
+                        start=(k == 0),
+                        stop=(k == PICKS - 1),
+                    )
+            else:
+                sums = work.tile([P, PARITIES * GROUPS], F32, name="sums_sbuf")
+                nc.vector.tensor_reduce(sums[:], by_group(products[:]), axis=AXIS.X, op=ALU.add)
             normed = work.tile([P, PARITIES * GROUPS], F32, name="normed")
-            nc.vector.tensor_reduce(normed[:], by_group(products[:]), axis=AXIS.X, op=ALU.add)
-            nc.vector.tensor_tensor(by_parity(normed[:]), by_parity(normed[:]), for_both(scale[:]), ALU.mult)
+            nc.vector.tensor_tensor(by_parity(normed[:]), by_parity(sums[:]), for_both(scale[:]), ALU.mult)
             nc.vector.tensor_tensor(by_parity(normed[:]), by_parity(normed[:]), for_both(shift[:]), ALU.add)
             swish = work.tile([P, PARITIES * GROUPS], F32, name="swish")
             nc.scalar.activation(swish[:], normed[:], ACT.Silu)

@@ -16,6 +16,7 @@ GROUPS = 64
 PICKS = 5
 N = GROUPS * PICKS
 BN_EPS = 1e-5
+WARM_UP = 6
 
 FLOPS = 2 * TRIALS * PARITIES * P * N
 BYTES = (
@@ -76,6 +77,9 @@ def tile_se_fbcnet_kernel(tc, x, w, conv_b, bn_gamma, bn_beta, bn_mean, bn_var, 
 
         identity = held.tile([P, P], F32, name="identity")
         make_identity(nc, identity[:])
+        unread = psum.tile([P, P], F32, name="unread")
+        for n in range(WARM_UP):
+            nc.tensor.matmul(unread[:], lhsT=identity[:], rhs=identity[:], start=True, stop=True)
 
         squares = held.tile([P, N], F32, name="squares")
         nc.scalar.activation(squares[:], weights[:], ACT.Square)

@@ -16,6 +16,7 @@ GROUPS = 64
 PICKS = 5
 N = GROUPS * PICKS
 BN_EPS = 1e-5
+TINY = 1e-30
 WARM_UP = 6
 
 FLOPS = 2 * TRIALS * PARITIES * P * N
@@ -85,14 +86,13 @@ def tile_se_fbcnet_kernel(tc, x, w, conv_b, bn_gamma, bn_beta, bn_mean, bn_var, 
         nc.scalar.activation(squares[:], weights[:], ACT.Square)
         limit = held.tile([P, GROUPS], F32, name="limit")
         nc.vector.tensor_reduce(limit[:], by_group(squares[:]), axis=AXIS.X, op=ALU.add)
-        nc.vector.tensor_scalar(limit[:], limit[:], 0.25, 1.0, op0=ALU.mult, op1=ALU.max)
-        nc.scalar.activation(limit[:], limit[:], ACT.Abs_reciprocal_sqrt)
+        nc.scalar.activation(limit[:], limit[:], ACT.Abs_reciprocal_sqrt, bias=TINY, scale=0.25)
 
         gain = held.tile([P, GROUPS], F32, name="gain")
         nc.scalar.activation(gain[:], var[:], ACT.Abs_reciprocal_sqrt, bias=BN_EPS)
         nc.vector.tensor_mul(gain[:], gain[:], gamma[:])
         scale = held.tile([P, GROUPS], F32, name="scale")
-        nc.vector.tensor_mul(scale[:], limit[:], gain[:])
+        nc.vector.scalar_tensor_tensor(scale[:], limit[:], 1.0, gain[:], op0=ALU.min, op1=ALU.mult)
         shift = held.tile([P, GROUPS], F32, name="shift")
         nc.vector.tensor_sub(shift[:], bias[:], mean[:])
         nc.vector.tensor_mul(shift[:], shift[:], gain[:])

@@ -17,7 +17,7 @@ PICKS = 5
 N = GROUPS * PICKS
 BN_EPS = 1e-5
 TINY = 1e-30
-WARM_UP = 6
+WARM_UP = 4
 
 FLOPS = 2 * TRIALS * PARITIES * P * N
 BYTES = (
@@ -64,16 +64,16 @@ def tile_se_fbcnet_kernel(tc, x, w, conv_b, bn_gamma, bn_beta, bn_mean, bn_var, 
         beta = held.tile([P, GROUPS], F32, name="beta")
 
         nc.scalar.dma_start(weights[:], block(w, 0, 0))
-        nc.scalar.dma_start(var[:], block(bn_var, 0, 0))
-        nc.scalar.dma_start(gamma[:], block(bn_gamma, 0, 0))
-        nc.scalar.dma_start(bias[:], block(conv_b, 0, 0))
 
         nc.sync.dma_start(offsets[:], offs)
         nc.sync.dma_start(windows[0][0][:], block(x, 0, 0))
         nc.sync.dma_start(windows[0][1][:], block(x, 0, 1))
-        nc.sync.dma_start(mean[:], block(bn_mean, 0, 0))
         nc.sync.dma_start(windows[1][0][:], block(x, 1, 0))
         nc.sync.dma_start(windows[1][1][:], block(x, 1, 1))
+        nc.sync.dma_start(var[:], block(bn_var, 0, 0))
+        nc.sync.dma_start(gamma[:], block(bn_gamma, 0, 0))
+        nc.sync.dma_start(bias[:], block(conv_b, 0, 0))
+        nc.sync.dma_start(mean[:], block(bn_mean, 0, 0))
         nc.sync.dma_start(beta[:], block(bn_beta, 0, 0))
 
         identity = held.tile([P, P], F32, name="identity")
@@ -84,9 +84,17 @@ def tile_se_fbcnet_kernel(tc, x, w, conv_b, bn_gamma, bn_beta, bn_mean, bn_var, 
 
         squares = held.tile([P, N], F32, name="squares")
         nc.scalar.activation(squares[:], weights[:], ACT.Square)
+        norms = psum.tile([P, GROUPS], F32, name="norms")
+        for k in range(PICKS):
+            nc.tensor.matmul(
+                norms[:],
+                lhsT=identity[:],
+                rhs=by_group(squares[:])[:, :, k],
+                start=(k == 0),
+                stop=(k == PICKS - 1),
+            )
         limit = held.tile([P, GROUPS], F32, name="limit")
-        nc.vector.tensor_reduce(limit[:], by_group(squares[:]), axis=AXIS.X, op=ALU.add)
-        nc.scalar.activation(limit[:], limit[:], ACT.Abs_reciprocal_sqrt, bias=TINY, scale=0.25)
+        nc.scalar.activation(limit[:], norms[:], ACT.Abs_reciprocal_sqrt, bias=TINY, scale=0.25)
 
         gain = held.tile([P, GROUPS], F32, name="gain")
         nc.scalar.activation(gain[:], var[:], ACT.Abs_reciprocal_sqrt, bias=BN_EPS)

@@ -44,11 +44,26 @@ def for_both(ap):
     return ap.unsqueeze(1).to_broadcast([P, PARITIES, GROUPS])
 
 
+def trial_rows(out, b):
+    rows = PARITIES * P
+    return out[b * rows : (b + 1) * rows, :].rearrange("(p i) q -> p (i q)", i=PARITIES)
+
+
+def add_fives(nc, sums, identity, terms):
+    for k in range(PICKS):
+        nc.tensor.matmul(
+            sums[:],
+            lhsT=identity[:],
+            rhs=by_group(terms[:])[:, :, k],
+            start=(k == 0),
+            stop=(k == PICKS - 1),
+        )
+
+
 def tile_se_fbcnet_kernel(tc, x, w, conv_b, bn_gamma, bn_beta, bn_mean, bn_var, offs, out):
     nc = tc.nc
     with (
         tc.tile_pool(name="held", bufs=1) as held,
-        tc.tile_pool(name="work", bufs=2) as work,
         tc.psum_pool(name="psum", bufs=1) as psum,
     ):
         offsets = held.tile([P, N // 16], U16, name="offsets")
@@ -64,16 +79,16 @@ def tile_se_fbcnet_kernel(tc, x, w, conv_b, bn_gamma, bn_beta, bn_mean, bn_var, 
         beta = held.tile([P, GROUPS], F32, name="beta")
 
         nc.scalar.dma_start(weights[:], block(w, 0, 0))
+        nc.scalar.dma_start(var[:], block(bn_var, 0, 0))
+        nc.scalar.dma_start(gamma[:], block(bn_gamma, 0, 0))
+        nc.scalar.dma_start(bias[:], block(conv_b, 0, 0))
 
         nc.sync.dma_start(offsets[:], offs)
         nc.sync.dma_start(windows[0][0][:], block(x, 0, 0))
         nc.sync.dma_start(windows[0][1][:], block(x, 0, 1))
+        nc.sync.dma_start(mean[:], block(bn_mean, 0, 0))
         nc.sync.dma_start(windows[1][0][:], block(x, 1, 0))
         nc.sync.dma_start(windows[1][1][:], block(x, 1, 1))
-        nc.sync.dma_start(var[:], block(bn_var, 0, 0))
-        nc.sync.dma_start(gamma[:], block(bn_gamma, 0, 0))
-        nc.sync.dma_start(bias[:], block(conv_b, 0, 0))
-        nc.sync.dma_start(mean[:], block(bn_mean, 0, 0))
         nc.sync.dma_start(beta[:], block(bn_beta, 0, 0))
 
         identity = held.tile([P, P], F32, name="identity")
@@ -82,58 +97,55 @@ def tile_se_fbcnet_kernel(tc, x, w, conv_b, bn_gamma, bn_beta, bn_mean, bn_var, 
         for n in range(WARM_UP):
             nc.tensor.matmul(unread[:], lhsT=identity[:], rhs=identity[:], start=True, stop=True)
 
-        squares = held.tile([P, N], F32, name="squares")
+        one = held.tile([P, 1], F32, name="one")
+        nc.vector.memset(one[:], 1.0)
+        unread_root = held.tile([P, 1], F32, name="unread_root")
+        nc.scalar.activation(unread_root[:], one[:], ACT.Abs_reciprocal_sqrt)
+
+        squares = held.tile([P, N], F32, name="squares", tag="squares")
         nc.scalar.activation(squares[:], weights[:], ACT.Square)
+        rstd = held.tile([P, GROUPS], F32, name="rstd")
+        nc.scalar.activation(rstd[:], var[:], ACT.Abs_reciprocal_sqrt, bias=BN_EPS)
         norms = psum.tile([P, GROUPS], F32, name="norms")
-        for k in range(PICKS):
-            nc.tensor.matmul(
-                norms[:],
-                lhsT=identity[:],
-                rhs=by_group(squares[:])[:, :, k],
-                start=(k == 0),
-                stop=(k == PICKS - 1),
-            )
+        add_fives(nc, norms, identity, squares)
         limit = held.tile([P, GROUPS], F32, name="limit")
         nc.scalar.activation(limit[:], norms[:], ACT.Abs_reciprocal_sqrt, bias=TINY, scale=0.25)
 
+        products_0 = held.tile([P, PARITIES * N], F32, name="products_0", tag="products_0")
+        products_1 = [held.tile([P, N], F32, name=f"products_1{i}") for i in range(PARITIES)]
+        sums_0 = psum.tile([P, PARITIES * GROUPS], F32, name="sums_0")
         gain = held.tile([P, GROUPS], F32, name="gain")
-        nc.scalar.activation(gain[:], var[:], ACT.Abs_reciprocal_sqrt, bias=BN_EPS)
-        nc.vector.tensor_mul(gain[:], gain[:], gamma[:])
-        scale = held.tile([P, GROUPS], F32, name="scale")
-        nc.vector.scalar_tensor_tensor(scale[:], limit[:], 1.0, gain[:], op0=ALU.min, op1=ALU.mult)
-        shift = held.tile([P, GROUPS], F32, name="shift")
-        nc.vector.tensor_sub(shift[:], bias[:], mean[:])
-        nc.vector.tensor_mul(shift[:], shift[:], gain[:])
-        nc.vector.tensor_add(shift[:], shift[:], beta[:])
-
-        for b in range(TRIALS):
-            products = work.tile([P, PARITIES * N], F32, name="products")
-            for i in range(PARITIES):
-                nc.vector.tensor_tensor(
-                    products[:, i * N : (i + 1) * N],
-                    windows[b][i][:].indirect(offsets[:]),
-                    weights[:],
-                    ALU.mult,
-                )
-            if b < TRIALS - 1:
-                sums = psum.tile([P, PARITIES * GROUPS], F32, name="sums_psum")
-                for k in range(PICKS):
-                    nc.tensor.matmul(
-                        sums[:],
-                        lhsT=identity[:],
-                        rhs=by_group(products[:])[:, :, k],
-                        start=(k == 0),
-                        stop=(k == PICKS - 1),
-                    )
-            else:
-                sums = work.tile([P, PARITIES * GROUPS], F32, name="sums_sbuf")
-                nc.vector.tensor_reduce(sums[:], by_group(products[:]), axis=AXIS.X, op=ALU.add)
-            normed = work.tile([P, PARITIES * GROUPS], F32, name="normed")
-            nc.vector.tensor_tensor(by_parity(normed[:]), by_parity(sums[:]), for_both(scale[:]), ALU.mult)
-            nc.vector.tensor_tensor(by_parity(normed[:]), by_parity(normed[:]), for_both(shift[:]), ALU.add)
-            swish = work.tile([P, PARITIES * GROUPS], F32, name="swish")
-            nc.scalar.activation(swish[:], normed[:], ACT.Silu)
-            nc.scalar.dma_start(
-                out[b * PARITIES * P : (b + 1) * PARITIES * P, :].rearrange("(p i) q -> p (i q)", i=PARITIES),
-                swish[:],
+        centre = held.tile([P, GROUPS], F32, name="centre")
+        for i in range(PARITIES):
+            nc.vector.tensor_tensor(
+                products_0[:, i * N : (i + 1) * N], windows[0][i][:].indirect(offsets[:]), weights[:], ALU.mult
             )
+        add_fives(nc, sums_0, identity, products_0)
+        nc.vector.tensor_mul(gain[:], rstd[:], gamma[:])
+        nc.vector.tensor_sub(centre[:], bias[:], mean[:])
+        for i in range(PARITIES):
+            nc.vector.tensor_tensor(products_1[i][:], windows[1][i][:].indirect(offsets[:]), weights[:], ALU.mult)
+
+        late = held.tile([P, N], F32, name="late", tag="squares")
+        sums_1 = late[:, : PARITIES * GROUPS]
+        scaled_centre = late[:, 2 * GROUPS : 3 * GROUPS]
+        shift = late[:, 3 * GROUPS : 4 * GROUPS]
+        scale = late[:, 4 * GROUPS : 5 * GROUPS]
+        scaled_0 = held.tile([P, PARITIES * GROUPS], F32, name="scaled_0")
+        normed_0 = held.tile([P, PARITIES * GROUPS], F32, name="normed_0")
+        scaled_1 = held.tile([P, PARITIES * GROUPS], F32, name="scaled_1", tag="products_0")
+        normed_1 = held.tile([P, PARITIES * GROUPS], F32, name="normed_1")
+        nc.vector.scalar_tensor_tensor(scale, limit[:], 1.0, gain[:], op0=ALU.min, op1=ALU.mult)
+        nc.vector.tensor_reduce(sums_1[:, :GROUPS], by_group(products_1[0][:]), axis=AXIS.X, op=ALU.add)
+        nc.vector.tensor_mul(scaled_centre, centre[:], gain[:])
+        nc.vector.tensor_reduce(sums_1[:, GROUPS:], by_group(products_1[1][:]), axis=AXIS.X, op=ALU.add)
+        nc.vector.tensor_add(shift, scaled_centre, beta[:])
+        nc.vector.tensor_tensor(by_parity(scaled_0[:]), by_parity(sums_0[:]), for_both(scale), ALU.mult)
+        nc.vector.tensor_tensor(by_parity(scaled_1[:]), by_parity(sums_1), for_both(scale), ALU.mult)
+        nc.vector.tensor_tensor(by_parity(normed_0[:]), by_parity(scaled_0[:]), for_both(shift), ALU.add)
+        nc.vector.tensor_tensor(by_parity(normed_1[:]), by_parity(scaled_1[:]), for_both(shift), ALU.add)
+
+        for b, normed in enumerate((normed_0, normed_1)):
+            swish = held.tile([P, PARITIES * GROUPS], F32, name=f"swish_{b}")
+            nc.scalar.activation(swish[:], normed[:], ACT.Silu)
+            nc.scalar.dma_start(trial_rows(out, b), swish[:])

@@ -86,9 +86,9 @@ def tile_se_fbcnet_kernel(tc, x, w, conv_b, bn_gamma, bn_beta, bn_mean, bn_var, 
         nc.sync.dma_start(offsets[:], offs)
         nc.sync.dma_start(windows[0][0][:], block(x, 0, 0))
         nc.sync.dma_start(windows[0][1][:], block(x, 0, 1))
-        nc.sync.dma_start(mean[:], block(bn_mean, 0, 0))
         nc.sync.dma_start(windows[1][0][:], block(x, 1, 0))
         nc.sync.dma_start(windows[1][1][:], block(x, 1, 1))
+        nc.sync.dma_start(mean[:], block(bn_mean, 0, 0))
         nc.sync.dma_start(beta[:], block(bn_beta, 0, 0))
 
         identity = held.tile([P, P], F32, name="identity")
@@ -115,29 +115,26 @@ def tile_se_fbcnet_kernel(tc, x, w, conv_b, bn_gamma, bn_beta, bn_mean, bn_var, 
         products_1 = [held.tile([P, N], F32, name=f"products_1{i}") for i in range(PARITIES)]
         sums_0 = psum.tile([P, PARITIES * GROUPS], F32, name="sums_0")
         gain = held.tile([P, GROUPS], F32, name="gain")
-        centre = held.tile([P, GROUPS], F32, name="centre")
         for i in range(PARITIES):
             nc.vector.tensor_tensor(
                 products_0[:, i * N : (i + 1) * N], windows[0][i][:].indirect(offsets[:]), weights[:], ALU.mult
             )
         add_fives(nc, sums_0, identity, products_0)
         nc.vector.tensor_mul(gain[:], rstd[:], gamma[:])
-        nc.vector.tensor_sub(centre[:], bias[:], mean[:])
         for i in range(PARITIES):
             nc.vector.tensor_tensor(products_1[i][:], windows[1][i][:].indirect(offsets[:]), weights[:], ALU.mult)
 
-        late = held.tile([P, N], F32, name="late", tag="squares")
+        late = held.tile([P, 6 * GROUPS], F32, name="late", tag="squares")
         sums_1 = late[:, : PARITIES * GROUPS]
-        scaled_centre = late[:, 2 * GROUPS : 3 * GROUPS]
-        shift = late[:, 3 * GROUPS : 4 * GROUPS]
-        scale = late[:, 4 * GROUPS : 5 * GROUPS]
+        scale, centre, scaled_centre, shift = (late[:, n * GROUPS : (n + 1) * GROUPS] for n in range(2, 6))
         scaled_0 = held.tile([P, PARITIES * GROUPS], F32, name="scaled_0")
         normed_0 = held.tile([P, PARITIES * GROUPS], F32, name="normed_0")
         scaled_1 = held.tile([P, PARITIES * GROUPS], F32, name="scaled_1", tag="products_0")
         normed_1 = held.tile([P, PARITIES * GROUPS], F32, name="normed_1")
         nc.vector.scalar_tensor_tensor(scale, limit[:], 1.0, gain[:], op0=ALU.min, op1=ALU.mult)
+        nc.vector.tensor_sub(centre, bias[:], mean[:])
         nc.vector.tensor_reduce(sums_1[:, :GROUPS], by_group(products_1[0][:]), axis=AXIS.X, op=ALU.add)
-        nc.vector.tensor_mul(scaled_centre, centre[:], gain[:])
+        nc.vector.tensor_mul(scaled_centre, centre, gain[:])
         nc.vector.tensor_reduce(sums_1[:, GROUPS:], by_group(products_1[1][:]), axis=AXIS.X, op=ALU.add)
         nc.vector.tensor_add(shift, scaled_centre, beta[:])
         nc.vector.tensor_tensor(by_parity(scaled_0[:]), by_parity(sums_0[:]), for_both(scale), ALU.mult)

@@ -111,7 +111,7 @@ def tile_se_fbcnet_kernel(tc, x, w, conv_b, bn_gamma, bn_beta, bn_mean, bn_var, 
         limit = held.tile([P, GROUPS], F32, name="limit")
         nc.scalar.activation(limit[:], norms[:], ACT.Abs_reciprocal_sqrt, bias=TINY, scale=0.25)
 
-        products_0 = held.tile([P, PARITIES * N], F32, name="products_0", tag="products_0")
+        products_0 = held.tile([P, PARITIES * N], F32, name="products_0")
         products_1 = [held.tile([P, N], F32, name=f"products_1{i}") for i in range(PARITIES)]
         sums_0 = psum.tile([P, PARITIES * GROUPS], F32, name="sums_0")
         gain = held.tile([P, GROUPS], F32, name="gain")
@@ -129,7 +129,7 @@ def tile_se_fbcnet_kernel(tc, x, w, conv_b, bn_gamma, bn_beta, bn_mean, bn_var, 
         scale, centre, scaled_centre, shift = (late[:, n * GROUPS : (n + 1) * GROUPS] for n in range(2, 6))
         scaled_0 = held.tile([P, PARITIES * GROUPS], F32, name="scaled_0")
         normed_0 = held.tile([P, PARITIES * GROUPS], F32, name="normed_0")
-        scaled_1 = held.tile([P, PARITIES * GROUPS], F32, name="scaled_1", tag="products_0")
+        scaled_1 = held.tile([P, PARITIES * GROUPS], F32, name="scaled_1")
         normed_1 = held.tile([P, PARITIES * GROUPS], F32, name="normed_1")
         nc.vector.scalar_tensor_tensor(scale, limit[:], 1.0, gain[:], op0=ALU.min, op1=ALU.mult)
         nc.vector.tensor_sub(centre, bias[:], mean[:])
@@ -137,12 +137,12 @@ def tile_se_fbcnet_kernel(tc, x, w, conv_b, bn_gamma, bn_beta, bn_mean, bn_var, 
         nc.vector.tensor_mul(scaled_centre, centre, gain[:])
         nc.vector.tensor_reduce(sums_1[:, GROUPS:], by_group(products_1[1][:]), axis=AXIS.X, op=ALU.add)
         nc.vector.tensor_add(shift, scaled_centre, beta[:])
-        nc.vector.tensor_tensor(by_parity(scaled_0[:]), by_parity(sums_0[:]), for_both(scale), ALU.mult)
         nc.vector.tensor_tensor(by_parity(scaled_1[:]), by_parity(sums_1), for_both(scale), ALU.mult)
-        nc.vector.tensor_tensor(by_parity(normed_0[:]), by_parity(scaled_0[:]), for_both(shift), ALU.add)
+        nc.vector.tensor_tensor(by_parity(scaled_0[:]), by_parity(sums_0[:]), for_both(scale), ALU.mult)
         nc.vector.tensor_tensor(by_parity(normed_1[:]), by_parity(scaled_1[:]), for_both(shift), ALU.add)
+        nc.vector.tensor_tensor(by_parity(normed_0[:]), by_parity(scaled_0[:]), for_both(shift), ALU.add)
 
-        for b, normed in enumerate((normed_0, normed_1)):
+        for b, normed in ((1, normed_1), (0, normed_0)):
             swish = held.tile([P, PARITIES * GROUPS], F32, name=f"swish_{b}")
             nc.scalar.activation(swish[:], normed[:], ACT.Silu)
             nc.scalar.dma_start(trial_rows(out, b), swish[:])

import concourse.mybir as mybir
from concourse.masks import make_identity

F32 = mybir.dt.float32
U16 = mybir.dt.uint16
ALU = mybir.AluOpType
ACT = mybir.ActivationFunctionType
AXIS = mybir.AxisListType

P = 128
TRIALS = 2
PARITIES = 2
BANDS = 8
ELECTRODES = 512
GROUPS = 64
PICKS = 5
N = GROUPS * PICKS
BN_EPS = 1e-5
TINY = 1e-30
WARM_UP = 4

FLOPS = 2 * TRIALS * PARITIES * P * N
BYTES = (
    TRIALS * PARITIES * P * ELECTRODES * 4
    + BANDS * (N + 5 * GROUPS) * 4
    + P * (N // 16) * 2
    + TRIALS * PARITIES * P * GROUPS * 4
)


def block(table, b, i):
    return table.rearrange("(b p i) n -> b i p n", b=TRIALS, i=PARITIES)[b, i]


def by_group(ap):
    return ap.rearrange("p (q k) -> p q k", k=PICKS)


def by_parity(ap):
    return ap.rearrange("p (i q) -> p i q", i=PARITIES)


def for_both(ap):
    return ap.unsqueeze(1).to_broadcast([P, PARITIES, GROUPS])


def trial_rows(out, b):
    rows = PARITIES * P
    return out[b * rows : (b + 1) * rows, :].rearrange("(p i) q -> p (i q)", i=PARITIES)


def add_fives(nc, sums, identity, terms):
    for k in range(PICKS):
        nc.tensor.matmul(
            sums[:],
            lhsT=identity[:],
            rhs=by_group(terms[:])[:, :, k],
            start=(k == 0),
            stop=(k == PICKS - 1),
        )


def tile_se_fbcnet_kernel(tc, x, w, conv_b, bn_gamma, bn_beta, bn_mean, bn_var, offs, out):
    nc = tc.nc
    with (
        tc.tile_pool(name="held", bufs=1) as held,
        tc.psum_pool(name="psum", bufs=1) as psum,
    ):
        offsets = held.tile([P, N // 16], U16, name="offsets")
        weights = held.tile([P, N], F32, name="weights")
        windows = [
            [held.tile([P, ELECTRODES], F32, name=f"window{b}{i}") for i in range(PARITIES)]
            for b in range(TRIALS)
        ]
        var = held.tile([P, GROUPS], F32, name="var")
        gamma = held.tile([P, GROUPS], F32, name="gamma")
        bias = held.tile([P, GROUPS], F32, name="bias")
        mean = held.tile([P, GROUPS], F32, name="mean")
        beta = held.tile([P, GROUPS], F32, name="beta")

        nc.scalar.dma_start(weights[:], block(w, 0, 0))
        nc.scalar.dma_start(var[:], block(bn_var, 0, 0))
        nc.scalar.dma_start(gamma[:], block(bn_gamma, 0, 0))
        nc.scalar.dma_start(bias[:], block(conv_b, 0, 0))

        nc.sync.dma_start(offsets[:], offs)
        nc.sync.dma_start(windows[0][0][:], block(x, 0, 0))
        nc.sync.dma_start(windows[0][1][:], block(x, 0, 1))
        nc.sync.dma_start(windows[1][0][:], block(x, 1, 0))
        nc.sync.dma_start(windows[1][1][:], block(x, 1, 1))
        nc.sync.dma_start(mean[:], block(bn_mean, 0, 0))
        nc.sync.dma_start(beta[:], block(bn_beta, 0, 0))

        identity = held.tile([P, P], F32, name="identity")
        make_identity(nc, identity[:])
        unread = psum.tile([P, P], F32, name="unread")
        for n in range(WARM_UP):
            nc.tensor.matmul(unread[:], lhsT=identity[:], rhs=identity[:], start=True, stop=True)

        one = held.tile([P, 1], F32, name="one")
        nc.vector.memset(one[:], 1.0)
        unread_root = held.tile([P, 1], F32, name="unread_root")
        nc.scalar.activation(unread_root[:], one[:], ACT.Abs_reciprocal_sqrt)

        squares = held.tile([P, N], F32, name="squares", tag="squares")
        nc.scalar.activation(squares[:], weights[:], ACT.Square)
        rstd = held.tile([P, GROUPS], F32, name="rstd")
        nc.scalar.activation(rstd[:], var[:], ACT.Abs_reciprocal_sqrt, bias=BN_EPS)
        norms = psum.tile([P, GROUPS], F32, name="norms")
        add_fives(nc, norms, identity, squares)
        limit = held.tile([P, GROUPS], F32, name="limit")
        nc.scalar.activation(limit[:], norms[:], ACT.Abs_reciprocal_sqrt, bias=TINY, scale=0.25)

        products_0 = held.tile([P, PARITIES * N], F32, name="products_0")
        products_1 = [held.tile([P, N], F32, name=f"products_1{i}") for i in range(PARITIES)]
        sums_0 = psum.tile([P, PARITIES * GROUPS], F32, name="sums_0")
        gain = held.tile([P, GROUPS], F32, name="gain")
        for i in range(PARITIES):
            nc.vector.tensor_tensor(
                products_0[:, i * N : (i + 1) * N], windows[0][i][:].indirect(offsets[:]), weights[:], ALU.mult
            )
        add_fives(nc, sums_0, identity, products_0)
        nc.vector.tensor_mul(gain[:], rstd[:], gamma[:])
        for i in range(PARITIES):
            nc.vector.tensor_tensor(products_1[i][:], windows[1][i][:].indirect(offsets[:]), weights[:], ALU.mult)

        late = held.tile([P, 6 * GROUPS], F32, name="late", tag="squares")
        sums_1 = late[:, : PARITIES * GROUPS]
        scale, centre, scaled_centre, shift = (late[:, n * GROUPS : (n + 1) * GROUPS] for n in range(2, 6))
        scaled_0 = held.tile([P, PARITIES * GROUPS], F32, name="scaled_0")
        normed_0 = held.tile([P, PARITIES * GROUPS], F32, name="normed_0")
        scaled_1 = held.tile([P, PARITIES * GROUPS], F32, name="scaled_1")
        normed_1 = held.tile([P, PARITIES * GROUPS], F32, name="normed_1")
        nc.vector.scalar_tensor_tensor(scale, limit[:], 1.0, gain[:], op0=ALU.min, op1=ALU.mult)
        nc.vector.tensor_sub(centre, bias[:], mean[:])
        nc.vector.tensor_reduce(sums_1[:, :GROUPS], by_group(products_1[0][:]), axis=AXIS.X, op=ALU.add)
        nc.vector.tensor_mul(scaled_centre, centre, gain[:])
        nc.vector.tensor_reduce(sums_1[:, GROUPS:], by_group(products_1[1][:]), axis=AXIS.X, op=ALU.add)
        nc.vector.tensor_add(shift, scaled_centre, beta[:])
        nc.vector.tensor_tensor(by_parity(scaled_1[:]), by_parity(sums_1), for_both(scale), ALU.mult)
        nc.vector.tensor_tensor(by_parity(scaled_0[:]), by_parity(sums_0[:]), for_both(scale), ALU.mult)
        nc.vector.tensor_tensor(by_parity(normed_1[:]), by_parity(scaled_1[:]), for_both(shift), ALU.add)
        nc.vector.tensor_tensor(by_parity(normed_0[:]), by_parity(scaled_0[:]), for_both(shift), ALU.add)

        for b, normed in ((1, normed_1), (0, normed_0)):
            swish = held.tile([P, PARITIES * GROUPS], F32, name=f"swish_{b}")
            nc.scalar.activation(swish[:], normed[:], ACT.Silu)
            nc.scalar.dma_start(trial_rows(out, b), swish[:])
